import numpy as np
import ml_dtypes


def mxq(x, axis, fmt="e4m3"):
    dtype, down = {"e4m3": (ml_dtypes.float8_e4m3fn, 7), "e5m2": (ml_dtypes.float8_e5m2, 14)}[fmt]
    v = np.moveaxis(np.asarray(x, np.float32).astype(ml_dtypes.bfloat16).astype(np.float64), axis, -1)
    blocks = v.reshape(v.shape[:-1] + (-1, 32))
    amax = np.abs(blocks).max(-1, keepdims=True)
    byte = np.maximum(np.where(amax > 0, np.frexp(amax)[1] - 1 + 127, 0) - down, 1)
    scale = np.exp2(byte - 127.0)
    codes = (blocks / scale).astype(np.float32).astype(dtype).astype(np.float64)
    return np.moveaxis((codes * scale).reshape(v.shape), -1, axis)


WIDE = False


def mx_kscale(k):
    if not WIDE:
        return np.ones(k)
    levels = np.array([10, -10, 5, -5, 0])
    if k % 512:
        return np.exp2(np.random.permutation(np.resize(levels, k // 32))).repeat(32)
    a = np.empty((k // 512, 16))
    for p in range(k // 512):
        a[p, :8] = np.random.permutation(np.resize(levels, 8))
        for g in range(8):
            far = levels[np.abs(levels - a[p, g]) >= 10]
            a[p, g + 8] = far[np.random.randint(len(far))]
    return np.exp2(a.ravel()).repeat(32)


BF16 = ml_dtypes.bfloat16


def bf(x):
    return np.asarray(x, np.float32).astype(BF16)


def f64(x):
    return np.asarray(x).astype(np.float64)


E2M1 = np.array([0.0, 0.5, 1.0, 1.5, 2.0, 3.0, 4.0, 6.0, -0.0, -0.5, -1.0, -1.5, -2.0, -3.0, -4.0, -6.0])


def pack_weight(w, fmt):
    k, n = w.shape
    w = f64(bf(w)).reshape(k // 32, 32, n)
    amax = np.abs(w).max(1)
    if fmt == "e4m3":
        byte = np.frexp(amax)[1] - 1 + 127 - 7
    else:
        mant, ex = np.frexp(amax / 6.0)
        byte = np.where(mant > 0.5, ex, ex - 1) + 127
    byte = np.clip(np.where(amax > 0, byte, 1), 1, 254)
    scaled = (w * np.exp2(127.0 - byte)[:, None, :]).reshape(k, n).astype(np.float32)
    by_word = np.ascontiguousarray(scaled.reshape(k // 512, 128, 4, n).transpose(0, 1, 3, 2))
    if fmt == "e4m3":
        words = by_word.astype(ml_dtypes.float8_e4m3fn).view(np.uint8)
    else:
        c = by_word.astype(ml_dtypes.float4_e2m1fn).view(np.uint8) & 0xF
        words = c[..., 0::2] | (c[..., 1::2] << 4)
    return np.ascontiguousarray(words), np.ascontiguousarray(byte.astype(np.uint8).reshape(k // 512, 16, n))


def unpack_weight(words, scales, fmt):
    g, p, n, _ = words.shape
    if fmt == "e4m3":
        vals = np.ascontiguousarray(words).view(ml_dtypes.float8_e4m3fn).astype(np.float64)
    else:
        nib = np.empty((g, p, n, 4), np.uint8)
        nib[..., 0::2] = words & 0xF
        nib[..., 1::2] = words >> 4
        vals = E2M1[nib]
    vals = vals * np.repeat(np.exp2(scales.astype(np.float64) - 127.0), 8, axis=1)[..., None]
    return vals.transpose(0, 1, 3, 2).reshape(g * 512, n)


B, S, N, D = 2, 1, 128, 4096


def setup_inputs():
    s, t = mx_kscale(D), mx_kscale(D)
    tensor0 = bf(np.random.standard_normal((S, N, D)) * s)
    tensor1 = bf(np.random.standard_normal((S, N, D)) * 0.5 / t)
    kernel = np.random.standard_normal((D, D)) * D ** -0.75 * t[:, None] / s[None, :]
    words, scales = pack_weight(np.ascontiguousarray(kernel.T), "e4m3")
    bias = bf(0.5 + 0.1 * np.random.standard_normal(1))
    return {"tensor0": tensor0,
            "tensor1": tensor1,
            "kernel_words": words,
            "kernel_scales": scales,
            "bias": bias}


def reference(tensor0, tensor1, kernel_words, kernel_scales, bias):
    q = mxq(f64(tensor0), 2, "e4m3") @ unpack_weight(kernel_words, kernel_scales, "e4m3")
    out = mxq(f64(tensor1), 2, "e4m3") @ mxq(q, 2, "e4m3").transpose(0, 2, 1)
    out = out + f64(bias)
    return np.ascontiguousarray(np.broadcast_to(out[None], (B,) + out.shape))

@@ -1,0 +1,217 @@
+from contextlib import ExitStack
+
+import concourse.mybir as mybir
+from concourse.masks import make_identity
+
+F32 = mybir.dt.float32
+BF16 = mybir.dt.bfloat16
+I32 = mybir.dt.int32
+U32 = mybir.dt.uint32
+U8 = mybir.dt.uint8
+FP8X4 = mybir.dt.float8_e4m3fn_x4
+
+P = 128
+D = 4096
+K_PASS = 512
+NG = D // K_PASS
+
+FLOPS = 2 * P * D * D + 2 * P * P * D
+
+
+def w_pieces():
+    whole = [(g, 0, D) for g in range(6)]
+    left = [(6, 0, D // 2), (7, 0, D // 2)]
+    right = [(6, D // 2, D // 2), (7, D // 2, D // 4), (7, 3 * D // 4, D // 4)]
+    return whole + left + right
+
+
+def tile_bilinear_w_kernel(tc, tensor0, tensor1, kernel_words, kernel_scales, bias, out):
+    nc = tc.nc
+    with ExitStack() as ctx:
+        keep = ctx.enter_context(tc.tile_pool(name="keep", bufs=1))
+        psum = ctx.enter_context(tc.psum_pool(name="psum", bufs=1))
+        ctx.enter_context(tc.manual_schedule())
+
+        def bank(i, shape, name):
+            return psum.tile(shape, F32, tag="bank%d" % i, name=name)
+
+        brow = keep.tile([P, 32], BF16)
+        nc.vector.memset(brow[:], 0.0)
+        wsc = keep.tile([P, 2, D], U8, align_bytes=64)
+        nc.vector.memset(wsc[:].rearrange("p h n -> p (h n)").bitcast(I32), 0)
+        ones = keep.tile([P, P], BF16)
+        nc.vector.memset(ones[:], 1.0)
+
+        ident32 = keep.tile([P, P], F32)
+        make_identity(nc, ident32[:])
+
+        t0_sb = keep.tile([P, D], BF16)
+        nc.sync.dma_start(out=t0_sb[:], in_=tensor0[0, :, :])
+        nc.sync.dma_start(out=brow[0:1, 0:1], in_=bias.unsqueeze(0))
+        t1_sb = {}
+
+        def load_t1(first_group, groups):
+            c0, c1 = K_PASS * first_group, K_PASS * (first_group + groups)
+            tile = keep.tile([P, c1 - c0], BF16, name="t1_%d" % first_group)
+            nc.sync.dma_start(out=tile[:], in_=tensor1[0, :, c0:c1])
+            for j in range(groups):
+                t1_sb[first_group + j] = (tile, K_PASS * j)
+
+        load_t1(0, 4)
+
+        ks = kernel_scales.bitcast(I32)
+        for h in range(2):
+            for half in range(2):
+                for quad in (0, 2, 1, 3):
+                    nc.sync.dma_start(
+                        out=wsc[32 * quad : 32 * quad + 16, h, 2048 * half : 2048 * (half + 1)].bitcast(I32),
+                        in_=ks[4 * h : 4 * h + 4, 4 * quad : 4 * quad + 4, 512 * half : 512 * (half + 1)],
+                    )
+
+        kw = kernel_words.rearrange("g p n t -> g p (n t)").bitcast(I32)
+        w_at = {}
+        for g, n0, cols in w_pieces():
+            wt = keep.tile([P, cols], U32, name="w%d_%d" % (g, n0), align_bytes=64)
+            nc.sync.dma_start(out=wt[:].bitcast(I32), in_=kw[g, :, n0 : n0 + cols])
+            for grp in range(n0 // K_PASS, (n0 + cols) // K_PASS):
+                w_at[(g, grp)] = (wt, K_PASS * grp - n0)
+
+        load_t1(4, 2)
+        load_t1(6, 2)
+
+        def transposes(b, pair, source, name):
+            xt = bank(b, [P, 2, 2, P], name)
+            for gg in range(2):
+                tile, c0 = source[2 * pair + gg]
+                words = tile[:].bitcast(F32)
+                for u in range(2):
+                    nc.tensor.transpose(
+                        out=xt[:, gg, u, :],
+                        in_=words[:, c0 // 2 + u : c0 // 2 + K_PASS // 2 : 2],
+                        identity=ident32[:],
+                    )
+            return xt
+
+        def lay_out(copy, grouped, pair, xt):
+            copy(
+                out=grouped[:].bitcast(F32)[:, 2 * pair : 2 * pair + 2, :, :],
+                in_=xt[:].rearrange("p g u j -> p g j u"),
+            )
+
+        def quantise(codes, scales, grouped, first, groups):
+            sl = slice(first, first + groups)
+            nc.vector.quantize_mx(
+                out=codes[:, sl, :].rearrange("p g j -> p (g j)").bitcast(FP8X4),
+                scales=scales[:, sl, :].rearrange("p g j -> p (g j)"),
+                in_=grouped[:, sl, :, :].rearrange("p g j t -> p (g j t)"),
+            )
+
+        def operand(name):
+            grouped = keep.tile([P, NG, P, 4], BF16, align_bytes=64, name=name + "g")
+            codes = keep.tile([P, NG, P], U32, align_bytes=64, name=name + "c")
+            scales = keep.tile([P, NG, P], U8, align_bytes=64, name=name + "s")
+            return grouped, codes, scales
+
+        t0g, t0c, t0s = operand("t0")
+        t1g, t1c, t1s = operand("t1")
+        qg, qc, qs = operand("q")
+
+        t0_at = {g: (t0_sb, K_PASS * g) for g in range(NG)}
+        for pair in range(4):
+            xt0 = transposes(pair, pair, t0_at, "xt0_%d" % pair)
+            lay_out(nc.vector.tensor_copy if pair % 2 == 0 else nc.scalar.copy, t0g, pair, xt0)
+        quantise(t0c, t0s, t0g, 0, 4)
+        quantise(t0c, t0s, t0g, 4, 4)
+
+        bps = bank(6, [P, 32], "bps")
+        nc.tensor.matmul(out=bps[:], lhsT=ones[:], rhs=brow[:], start=True, stop=True)
+        bias32 = keep.tile([P, 1], F32)
+        nc.scalar.copy(out=bias32[:], in_=bps[:, 0:1])
+
+        for pair in range(2):
+            xt1 = transposes(4 + pair, pair, t1_sb, "xt1_%d" % pair)
+            lay_out(nc.scalar.copy if pair % 2 == 0 else nc.vector.tensor_copy, t1g, pair, xt1)
+        quantise(t1c, t1s, t1g, 0, 4)
+
+        qps = [bank(grp, [P, K_PASS], "qps%d" % grp) for grp in range(NG)]
+
+        def passes(g, groups):
+            for grp in groups:
+                wt, off = w_at[(g, grp)]
+                n = K_PASS * grp
+                nc.tensor.matmul_mx(
+                    out=qps[grp][:],
+                    lhsT=t0c[:, g, :].bitcast(FP8X4),
+                    lhsT_scale=t0s[:, g, :],
+                    rhs=wt[:, off : off + K_PASS].bitcast(FP8X4),
+                    rhs_scale=wsc[4 * (g % 4) : P, g // 4, n : n + K_PASS],
+                    start=(g == 0),
+                    stop=(g == NG - 1),
+                )
+
+        q_sb = {}
+
+        def copy_out(grp):
+            qb = keep.tile([P, K_PASS], BF16, name="q%d" % grp)
+            copy = nc.scalar.copy if grp % 2 == 0 else nc.vector.tensor_copy
+            copy(out=qb[:], in_=qps[grp][:])
+            q_sb[grp] = (qb, 0)
+
+        accs = []
+
+        def second_stage(groups):
+            for grp in groups:
+                nc.tensor.matmul_mx(
+                    out=accs[0][:],
+                    lhsT=t1c[:, grp, :].bitcast(FP8X4),
+                    lhsT_scale=t1s[:, grp, :],
+                    rhs=qc[:, grp, :].bitcast(FP8X4),
+                    rhs_scale=qs[:, grp, :],
+                    start=(grp == 0),
+                    stop=(grp == NG - 1),
+                )
+
+        for g in range(6):
+            passes(g, range(NG))
+        passes(6, range(4))
+        passes(7, range(4))
+        for grp in range(4):
+            copy_out(grp)
+        xq01 = transposes(0, 0, q_sb, "xq01")
+        xq23 = transposes(1, 1, q_sb, "xq23")
+        lay_out(nc.scalar.copy, qg, 0, xq01)
+        lay_out(nc.vector.tensor_copy, qg, 1, xq23)
+        quantise(qc, qs, qg, 0, 2)
+        quantise(qc, qs, qg, 2, 2)
+
+        passes(6, range(4, 8))
+        acc = bank(2, [P, P], "acc")
+        accs.append(acc)
+        second_stage(range(4))
+
+        passes(7, (4, 5))
+        copy_out(4)
+        copy_out(5)
+        xq45 = transposes(3, 2, q_sb, "xq45")
+        lay_out(nc.scalar.copy, qg, 2, xq45)
+        quantise(qc, qs, qg, 4, 2)
+
+        passes(7, (6, 7))
+        copy_out(6)
+        copy_out(7)
+        xt45 = transposes(0, 2, t1_sb, "xt1_2")
+        lay_out(nc.scalar.copy, t1g, 2, xt45)
+        xq67 = transposes(1, 3, q_sb, "xq67")
+        lay_out(nc.vector.tensor_copy, qg, 3, xq67)
+        quantise(t1c, t1s, t1g, 4, 2)
+        xt67 = transposes(4, 3, t1_sb, "xt1_3")
+        lay_out(nc.scalar.copy, t1g, 3, xt67)
+        quantise(qc, qs, qg, 6, 2)
+        second_stage((4, 5))
+        quantise(t1c, t1s, t1g, 6, 2)
+        second_stage((6, 7))
+
+        res = keep.tile([P, P], F32)
+        nc.vector.tensor_scalar_add(out=res[:], in0=acc[:], scalar1=bias32[:, 0:1])
+        nc.sync.dma_start(out=out[0, 0, :, :], in_=res[:])
+        nc.scalar.dma_start(out=out[1, 0, :, :], in_=res[:])

@@ -20,9 +20,10 @@ FLOPS = 2 * P * D * D + 2 * P * P * D
 
 def w_pieces():
     whole = [(g, 0, D) for g in range(6)]
-    left = [(6, 0, D // 2), (7, 0, D // 2)]
-    right = [(6, D // 2, D // 2), (7, D // 2, D // 4), (7, 3 * D // 4, D // 4)]
-    return whole + left + right
+    left = [(6, 0, 2048), (7, 0, 2048)]
+    middle = [(6, 2048, 1024), (7, 2048, 1024)]
+    right = [(6, 3072, 1024), (7, 3072, 512), (7, 3584, 512)]
+    return whole + left + middle + right
 
 
 def tile_bilinear_w_kernel(tc, tensor0, tensor1, kernel_words, kernel_scales, bias, out):
@@ -48,16 +49,8 @@ def tile_bilinear_w_kernel(tc, tensor0, tensor1, kernel_words, kernel_scales, bi
         t0_sb = keep.tile([P, D], BF16)
         nc.sync.dma_start(out=t0_sb[:], in_=tensor0[0, :, :])
         nc.sync.dma_start(out=brow[0:1, 0:1], in_=bias.unsqueeze(0))
-        t1_sb = {}
-
-        def load_t1(first_group, groups):
-            c0, c1 = K_PASS * first_group, K_PASS * (first_group + groups)
-            tile = keep.tile([P, c1 - c0], BF16, name="t1_%d" % first_group)
-            nc.sync.dma_start(out=tile[:], in_=tensor1[0, :, c0:c1])
-            for j in range(groups):
-                t1_sb[first_group + j] = (tile, K_PASS * j)
-
-        load_t1(0, 4)
+        t1_sb = keep.tile([P, D], BF16)
+        nc.sync.dma_start(out=t1_sb[:], in_=tensor1[0, :, :])
 
         ks = kernel_scales.bitcast(I32)
         for h in range(2):
@@ -76,25 +69,22 @@ def tile_bilinear_w_kernel(tc, tensor0, tensor1, kernel_words, kernel_scales, bi
             for grp in range(n0 // K_PASS, (n0 + cols) // K_PASS):
                 w_at[(g, grp)] = (wt, K_PASS * grp - n0)
 
-        load_t1(4, 2)
-        load_t1(6, 2)
-
-        def transposes(b, pair, source, name):
-            xt = bank(b, [P, 2, 2, P], name)
-            for gg in range(2):
-                tile, c0 = source[2 * pair + gg]
+        def transposes(b, groups, source, name):
+            xt = bank(b, [P, len(groups), 2, P], name)
+            for i, grp in enumerate(groups):
+                tile, c0 = source[grp]
                 words = tile[:].bitcast(F32)
                 for u in range(2):
                     nc.tensor.transpose(
-                        out=xt[:, gg, u, :],
+                        out=xt[:, i, u, :],
                         in_=words[:, c0 // 2 + u : c0 // 2 + K_PASS // 2 : 2],
                         identity=ident32[:],
                     )
             return xt
 
-        def lay_out(copy, grouped, pair, xt):
+        def lay_out(copy, grouped, groups, xt):
             copy(
-                out=grouped[:].bitcast(F32)[:, 2 * pair : 2 * pair + 2, :, :],
+                out=grouped[:].bitcast(F32)[:, groups[0] : groups[0] + len(groups), :, :],
                 in_=xt[:].rearrange("p g u j -> p g j u"),
             )
 
@@ -116,10 +106,12 @@ def tile_bilinear_w_kernel(tc, tensor0, tensor1, kernel_words, kernel_scales, bi
         t1g, t1c, t1s = operand("t1")
         qg, qc, qs = operand("q")
 
+        vcopy, scopy = nc.vector.tensor_copy, nc.scalar.copy
         t0_at = {g: (t0_sb, K_PASS * g) for g in range(NG)}
         for pair in range(4):
-            xt0 = transposes(pair, pair, t0_at, "xt0_%d" % pair)
-            lay_out(nc.vector.tensor_copy if pair % 2 == 0 else nc.scalar.copy, t0g, pair, xt0)
+            groups = (2 * pair, 2 * pair + 1)
+            xt0 = transposes(pair, groups, t0_at, "xt0_%d" % pair)
+            lay_out(vcopy if pair % 2 == 0 else scopy, t0g, groups, xt0)
         quantise(t0c, t0s, t0g, 0, 4)
         quantise(t0c, t0s, t0g, 4, 4)
 
@@ -128,10 +120,13 @@ def tile_bilinear_w_kernel(tc, tensor0, tensor1, kernel_words, kernel_scales, bi
         bias32 = keep.tile([P, 1], F32)
         nc.scalar.copy(out=bias32[:], in_=bps[:, 0:1])
 
-        for pair in range(2):
-            xt1 = transposes(4 + pair, pair, t1_sb, "xt1_%d" % pair)
-            lay_out(nc.scalar.copy if pair % 2 == 0 else nc.vector.tensor_copy, t1g, pair, xt1)
+        t1_at = {g: (t1_sb, K_PASS * g) for g in range(NG)}
+        for pair, b in enumerate((4, 5, 7, 0)):
+            groups = (2 * pair, 2 * pair + 1)
+            xt1 = transposes(b, groups, t1_at, "xt1_%d" % pair)
+            lay_out(scopy if pair % 2 == 0 else vcopy, t1g, groups, xt1)
         quantise(t1c, t1s, t1g, 0, 4)
+        quantise(t1c, t1s, t1g, 4, 4)
 
         qps = [bank(grp, [P, K_PASS], "qps%d" % grp) for grp in range(NG)]
 
@@ -153,7 +148,7 @@ def tile_bilinear_w_kernel(tc, tensor0, tensor1, kernel_words, kernel_scales, bi
 
         def copy_out(grp):
             qb = keep.tile([P, K_PASS], BF16, name="q%d" % grp)
-            copy = nc.scalar.copy if grp % 2 == 0 else nc.vector.tensor_copy
+            copy = scopy if grp % 2 == 0 else vcopy
             copy(out=qb[:], in_=qps[grp][:])
             q_sb[grp] = (qb, 0)
 
@@ -177,38 +172,38 @@ def tile_bilinear_w_kernel(tc, tensor0, tensor1, kernel_words, kernel_scales, bi
         passes(7, range(4))
         for grp in range(4):
             copy_out(grp)
-        xq01 = transposes(0, 0, q_sb, "xq01")
-        xq23 = transposes(1, 1, q_sb, "xq23")
-        lay_out(nc.scalar.copy, qg, 0, xq01)
-        lay_out(nc.vector.tensor_copy, qg, 1, xq23)
+        xq01 = transposes(0, (0, 1), q_sb, "xq01")
+        xq23 = transposes(1, (2, 3), q_sb, "xq23")
+        lay_out(scopy, qg, (0, 1), xq01)
+        lay_out(vcopy, qg, (2, 3), xq23)
         quantise(qc, qs, qg, 0, 2)
         quantise(qc, qs, qg, 2, 2)
 
-        passes(6, range(4, 8))
-        acc = bank(2, [P, P], "acc")
-        accs.append(acc)
-        second_stage(range(4))
-
+        passes(6, (4, 5))
         passes(7, (4, 5))
         copy_out(4)
         copy_out(5)
-        xq45 = transposes(3, 2, q_sb, "xq45")
-        lay_out(nc.scalar.copy, qg, 2, xq45)
-        quantise(qc, qs, qg, 4, 2)
+        acc = bank(2, [P, P], "acc")
+        accs.append(acc)
+        second_stage(range(4))
+        xq4 = transposes(3, (4,), q_sb, "xq4")
+        xq5 = transposes(0, (5,), q_sb, "xq5")
+        lay_out(scopy, qg, (4,), xq4)
+        lay_out(vcopy, qg, (5,), xq5)
 
-        passes(7, (6, 7))
+        passes(6, (6, 7))
+        passes(7, (6,))
         copy_out(6)
+        quantise(qc, qs, qg, 4, 2)
+        passes(7, (7,))
         copy_out(7)
-        xt45 = transposes(0, 2, t1_sb, "xt1_2")
-        lay_out(nc.scalar.copy, t1g, 2, xt45)
-        xq67 = transposes(1, 3, q_sb, "xq67")
-        lay_out(nc.vector.tensor_copy, qg, 3, xq67)
-        quantise(t1c, t1s, t1g, 4, 2)
-        xt67 = transposes(4, 3, t1_sb, "xt1_3")
-        lay_out(nc.scalar.copy, t1g, 3, xt67)
-        quantise(qc, qs, qg, 6, 2)
+        xq6 = transposes(1, (6,), q_sb, "xq6")
+        lay_out(scopy, qg, (6,), xq6)
         second_stage((4, 5))
-        quantise(t1c, t1s, t1g, 6, 2)
+        xq7 = transposes(4, (7,), q_sb, "xq7")
+        lay_out(scopy, qg, (7,), xq7)
+        quantise(qc, qs, qg, 6, 1)
+        quantise(qc, qs, qg, 7, 1)
         second_stage((6, 7))
 
         res = keep.tile([P, P], F32)

@@ -19,9 +19,9 @@ FLOPS = 2 * P * D * D + 2 * P * P * D
 
 
 def w_pieces():
-    whole = [(g, 0, D) for g in range(6)]
-    left = [(6, 0, 2048), (7, 0, 2048)]
-    middle = [(6, 2048, 1024), (7, 2048, 1024)]
+    whole = [(g, 0, D) for g in range(4)]
+    left = [(g, 0, 2048) for g in range(4, 8)]
+    middle = [(4, 2048, 2048), (5, 2048, 2048), (6, 2048, 1024), (7, 2048, 1024)]
     right = [(6, 3072, 1024), (7, 3072, 512), (7, 3584, 512)]
     return whole + left + middle + right
 
@@ -128,29 +128,43 @@ def tile_bilinear_w_kernel(tc, tensor0, tensor1, kernel_words, kernel_scales, bi
         quantise(t1c, t1s, t1g, 0, 4)
         quantise(t1c, t1s, t1g, 4, 4)
 
-        qps = [bank(grp, [P, K_PASS], "qps%d" % grp) for grp in range(NG)]
+        last = NG - 1
+        half = K_PASS // 2
+        qps = [bank(grp, [P, K_PASS], "qps%d" % grp) for grp in range(last)]
+        q_last = []
+
+        def one_pass(out, g, grp, n0, cols):
+            wt, off = w_at[(g, grp)]
+            n = K_PASS * grp + n0
+            nc.tensor.matmul_mx(
+                out=out,
+                lhsT=t0c[:, g, :].bitcast(FP8X4),
+                lhsT_scale=t0s[:, g, :],
+                rhs=wt[:, off + n0 : off + n0 + cols].bitcast(FP8X4),
+                rhs_scale=wsc[4 * (g % 4) : P, g // 4, n : n + cols],
+                start=(g == 0),
+                stop=(g == NG - 1),
+            )
 
         def passes(g, groups):
             for grp in groups:
-                wt, off = w_at[(g, grp)]
-                n = K_PASS * grp
-                nc.tensor.matmul_mx(
-                    out=qps[grp][:],
-                    lhsT=t0c[:, g, :].bitcast(FP8X4),
-                    lhsT_scale=t0s[:, g, :],
-                    rhs=wt[:, off : off + K_PASS].bitcast(FP8X4),
-                    rhs_scale=wsc[4 * (g % 4) : P, g // 4, n : n + K_PASS],
-                    start=(g == 0),
-                    stop=(g == NG - 1),
-                )
+                one_pass(qps[grp][:], g, grp, 0, K_PASS)
+
+        def passes_last(g):
+            for i in range(2):
+                one_pass(q_last[i][:], g, last, half * i, half)
 
         q_sb = {}
 
         def copy_out(grp):
             qb = keep.tile([P, K_PASS], BF16, name="q%d" % grp)
-            copy = scopy if grp % 2 == 0 else vcopy
-            copy(out=qb[:], in_=qps[grp][:])
             q_sb[grp] = (qb, 0)
+            if grp < last:
+                copy = scopy if grp % 2 == 0 else vcopy
+                copy(out=qb[:], in_=qps[grp][:])
+            else:
+                scopy(out=qb[:, :half], in_=q_last[0][:])
+                vcopy(out=qb[:, half:], in_=q_last[1][:])
 
         accs = []
 
@@ -166,42 +180,51 @@ def tile_bilinear_w_kernel(tc, tensor0, tensor1, kernel_words, kernel_scales, bi
                     stop=(grp == NG - 1),
                 )
 
-        for g in range(6):
-            passes(g, range(NG))
-        passes(6, range(4))
-        passes(7, range(4))
+        for g in range(4):
+            passes(g, range(last))
+        for g in range(4, NG):
+            passes(g, range(4))
         for grp in range(4):
             copy_out(grp)
+        for i, b in enumerate((3, 7)):
+            ql = bank(b, [P, half], "q_last%d" % i)
+            q_last.append(ql)
+        for g in range(4):
+            passes_last(g)
+        passes(4, range(4, last))
+        passes_last(4)
         xq01 = transposes(0, (0, 1), q_sb, "xq01")
         xq23 = transposes(1, (2, 3), q_sb, "xq23")
         lay_out(scopy, qg, (0, 1), xq01)
         lay_out(vcopy, qg, (2, 3), xq23)
         quantise(qc, qs, qg, 0, 2)
         quantise(qc, qs, qg, 2, 2)
+        passes(5, range(4, last))
+        passes_last(5)
+        acc = bank(2, [P, P], "acc")
+        accs.append(acc)
+        second_stage(range(4))
 
         passes(6, (4, 5))
         passes(7, (4, 5))
         copy_out(4)
         copy_out(5)
-        acc = bank(2, [P, P], "acc")
-        accs.append(acc)
-        second_stage(range(4))
-        xq4 = transposes(3, (4,), q_sb, "xq4")
-        xq5 = transposes(0, (5,), q_sb, "xq5")
-        lay_out(scopy, qg, (4,), xq4)
-        lay_out(vcopy, qg, (5,), xq5)
-
-        passes(6, (6, 7))
+        passes(6, (6,))
+        passes_last(6)
         passes(7, (6,))
         copy_out(6)
-        quantise(qc, qs, qg, 4, 2)
-        passes(7, (7,))
+        xq4 = transposes(0, (4,), q_sb, "xq4")
+        xq5 = transposes(1, (5,), q_sb, "xq5")
+        lay_out(scopy, qg, (4,), xq4)
+        lay_out(vcopy, qg, (5,), xq5)
+        passes_last(7)
         copy_out(7)
-        xq6 = transposes(1, (6,), q_sb, "xq6")
+        quantise(qc, qs, qg, 4, 2)
+        xq6 = transposes(4, (6,), q_sb, "xq6")
         lay_out(scopy, qg, (6,), xq6)
-        second_stage((4, 5))
-        xq7 = transposes(4, (7,), q_sb, "xq7")
+        xq7 = transposes(5, (7,), q_sb, "xq7")
         lay_out(scopy, qg, (7,), xq7)
+        second_stage((4, 5))
         quantise(qc, qs, qg, 6, 1)
         quantise(qc, qs, qg, 7, 1)
         second_stage((6, 7))

@@ -18,23 +18,18 @@ NG = D // K_PASS
 FLOPS = 2 * P * D * D + 2 * P * P * D
 
 
-def w_pieces():
-    whole = [(g, 0, D) for g in range(4)]
-    left = [(g, 0, 2048) for g in range(4, 8)]
-    middle = [(4, 2048, 2048), (5, 2048, 2048), (6, 2048, 1024), (7, 2048, 1024)]
-    right = [(6, 3072, 1024), (7, 3072, 512), (7, 3584, 512)]
-    return whole + left + middle + right
-
-
 def tile_bilinear_w_kernel(tc, tensor0, tensor1, kernel_words, kernel_scales, bias, out):
     nc = tc.nc
     with ExitStack() as ctx:
         keep = ctx.enter_context(tc.tile_pool(name="keep", bufs=1))
+        raw = ctx.enter_context(tc.tile_pool(name="raw", bufs=5))
+        sorted_w = ctx.enter_context(tc.tile_pool(name="sorted", bufs=4))
         psum = ctx.enter_context(tc.psum_pool(name="psum", bufs=1))
         ctx.enter_context(tc.manual_schedule())
+        vcopy, scopy = nc.vector.tensor_copy, nc.scalar.copy
 
-        def bank(i, shape, name):
-            return psum.tile(shape, F32, tag="bank%d" % i, name=name)
+        def bank(i, shape, name, dtype=F32):
+            return psum.tile(shape, dtype, tag="bank%d" % i, name=name)
 
         brow = keep.tile([P, 32], BF16)
         nc.vector.memset(brow[:], 0.0)
@@ -45,6 +40,8 @@ def tile_bilinear_w_kernel(tc, tensor0, tensor1, kernel_words, kernel_scales, bi
 
         ident32 = keep.tile([P, P], F32)
         make_identity(nc, ident32[:])
+        identb = keep.tile([P, P], BF16)
+        make_identity(nc, identb[:])
 
         t0_sb = keep.tile([P, D], BF16)
         nc.sync.dma_start(out=t0_sb[:], in_=tensor0[0, :, :])
@@ -62,31 +59,26 @@ def tile_bilinear_w_kernel(tc, tensor0, tensor1, kernel_words, kernel_scales, bi
                     )
 
         kw = kernel_words.rearrange("g p n t -> g p (n t)").bitcast(I32)
-        w_at = {}
-        for g, n0, cols in w_pieces():
-            wt = keep.tile([P, cols], U32, name="w%d_%d" % (g, n0), align_bytes=64)
-            nc.sync.dma_start(out=wt[:].bitcast(I32), in_=kw[g, :, n0 : n0 + cols])
-            for grp in range(n0 // K_PASS, (n0 + cols) // K_PASS):
-                w_at[(g, grp)] = (wt, K_PASS * grp - n0)
+        w_raw = {}
 
-        def transposes(b, groups, source, name):
-            xt = bank(b, [P, len(groups), 2, P], name)
-            for i, grp in enumerate(groups):
-                tile, c0 = source[grp]
-                words = tile[:].bitcast(F32)
-                for u in range(2):
-                    nc.tensor.transpose(
-                        out=xt[:, i, u, :],
-                        in_=words[:, c0 // 2 + u : c0 // 2 + K_PASS // 2 : 2],
-                        identity=ident32[:],
-                    )
-            return xt
+        def load_w(g, first_group, groups):
+            n0, cols = K_PASS * first_group, K_PASS * groups
+            wt = raw.tile([P, cols], I32, tag="raw", name="w%d_%d" % (g, first_group), align_bytes=64)
+            nc.sync.dma_start(out=wt[:], in_=kw[g, :, n0 : n0 + cols])
+            for j in range(groups):
+                w_raw[(g, first_group + j)] = (wt, K_PASS * j)
 
-        def lay_out(copy, grouped, groups, xt):
-            copy(
-                out=grouped[:].bitcast(F32)[:, groups[0] : groups[0] + len(groups), :, :],
-                in_=xt[:].rearrange("p g u j -> p g j u"),
-            )
+        for g in range(4):
+            load_w(g, 0, 8)
+        for g in range(4, NG):
+            load_w(g, 0, 4)
+        for g in (4, 5):
+            load_w(g, 4, 4)
+        for g in (6, 7):
+            load_w(g, 4, 2)
+        load_w(6, 6, 2)
+        load_w(7, 6, 1)
+        load_w(7, 7, 1)
 
         def quantise(codes, scales, grouped, first, groups):
             sl = slice(first, first + groups)
@@ -106,65 +98,78 @@ def tile_bilinear_w_kernel(tc, tensor0, tensor1, kernel_words, kernel_scales, bi
         t1g, t1c, t1s = operand("t1")
         qg, qc, qs = operand("q")
 
-        vcopy, scopy = nc.vector.tensor_copy, nc.scalar.copy
-        t0_at = {g: (t0_sb, K_PASS * g) for g in range(NG)}
+        words = t0_sb[:].bitcast(F32)
         for pair in range(4):
-            groups = (2 * pair, 2 * pair + 1)
-            xt0 = transposes(pair, groups, t0_at, "xt0_%d" % pair)
-            lay_out(vcopy if pair % 2 == 0 else scopy, t0g, groups, xt0)
+            xt0 = bank(pair, [P, 2, 2, P], "xt0_%d" % pair)
+            for i in range(2):
+                w0 = 256 * (2 * pair + i)
+                for u in range(2):
+                    nc.tensor.transpose(out=xt0[:, i, u, :], in_=words[:, w0 + u : w0 + 256 : 2], identity=ident32[:])
+            copy = vcopy if pair % 2 == 0 else scopy
+            copy(
+                out=t0g[:].bitcast(F32)[:, 2 * pair : 2 * pair + 2, :, :],
+                in_=xt0[:].rearrange("p g u j -> p g j u"),
+            )
         quantise(t0c, t0s, t0g, 0, 4)
         quantise(t0c, t0s, t0g, 4, 4)
 
         bps = bank(6, [P, 32], "bps")
         nc.tensor.matmul(out=bps[:], lhsT=ones[:], rhs=brow[:], start=True, stop=True)
         bias32 = keep.tile([P, 1], F32)
-        nc.scalar.copy(out=bias32[:], in_=bps[:, 0:1])
+        scopy(out=bias32[:], in_=bps[:, 0:1])
 
-        t1_at = {g: (t1_sb, K_PASS * g) for g in range(NG)}
+        t1_sorted = keep.tile([P, 4, P, 4], F32)
+        vcopy(out=t1_sorted[:], in_=t1_sb[:].bitcast(F32).rearrange("p (b t r) -> p t b r", t=4, r=4))
+        t1_cols = t1_sorted[:].rearrange("p t b r -> p (t b r)").bitcast(BF16)
         for pair, b in enumerate((4, 5, 7, 0)):
-            groups = (2 * pair, 2 * pair + 1)
-            xt1 = transposes(b, groups, t1_at, "xt1_%d" % pair)
-            lay_out(scopy if pair % 2 == 0 else vcopy, t1g, groups, xt1)
+            xt1 = bank(b, [P, 2, 4, P], "xt1_%d" % pair, BF16)
+            for i in range(2):
+                for t in range(4):
+                    c0 = D // 4 * t + P * (2 * pair + i)
+                    nc.tensor.transpose(out=xt1[:, i, t, :], in_=t1_cols[:, c0 : c0 + P], identity=identb[:])
+            copy = scopy if pair % 2 == 0 else vcopy
+            copy(out=t1g[:, 2 * pair : 2 * pair + 2, :, :], in_=xt1[:].rearrange("p g t i -> p g i t"))
         quantise(t1c, t1s, t1g, 0, 4)
         quantise(t1c, t1s, t1g, 4, 4)
 
-        last = NG - 1
-        half = K_PASS // 2
-        qps = [bank(grp, [P, K_PASS], "qps%d" % grp) for grp in range(last)]
-        q_last = []
-
-        def one_pass(out, g, grp, n0, cols):
-            wt, off = w_at[(g, grp)]
-            n = K_PASS * grp + n0
-            nc.tensor.matmul_mx(
-                out=out,
-                lhsT=t0c[:, g, :].bitcast(FP8X4),
-                lhsT_scale=t0s[:, g, :],
-                rhs=wt[:, off + n0 : off + n0 + cols].bitcast(FP8X4),
-                rhs_scale=wsc[4 * (g % 4) : P, g // 4, n : n + cols],
-                start=(g == 0),
-                stop=(g == NG - 1),
+        wss = keep.tile([P, 2, 4, D // 4], U8, align_bytes=64)
+        for h in range(2):
+            vcopy(
+                out=wss[:, h, :, :].rearrange("p t c -> p (t c)").bitcast(I32).rearrange("p (t b r) -> p t b r", t=4, r=2),
+                in_=wsc[:, h, :].bitcast(I32).rearrange("p (b t r) -> p t b r", t=4, r=2),
             )
+
+        w_at = {}
+
+        def sort_w(g, first_group, groups):
+            wt, off = w_raw[(g, first_group)]
+            cols = P * groups
+            ws = sorted_w.tile([P, 4, cols], I32, tag="s%d" % groups, name="s%d_%d" % (g, first_group), align_bytes=64)
+            vcopy(
+                out=ws[:].rearrange("p t (b r) -> p t b r", r=8),
+                in_=wt[:, off : off + 4 * cols].rearrange("p (b t r) -> p t b r", t=4, r=8),
+            )
+            for j in range(groups):
+                w_at[(g, first_group + j)] = (ws, P * j)
+
+        qps = [bank(grp, [P, 4, P], "qps%d" % grp) for grp in range(NG)]
 
         def passes(g, groups):
             for grp in groups:
-                one_pass(qps[grp][:], g, grp, 0, K_PASS)
+                ws, c0 = w_at[(g, grp)]
+                for t in range(4):
+                    nc.tensor.matmul_mx(
+                        out=qps[grp][:, t, :],
+                        lhsT=ws[:, t, c0 : c0 + P].bitcast(FP8X4),
+                        lhsT_scale=wss[4 * (g % 4) : P, g // 4, t, P * grp : P * (grp + 1)],
+                        rhs=t0c[:, g, :].bitcast(FP8X4),
+                        rhs_scale=t0s[:, g, :],
+                        start=(g == 0 and t == 0),
+                        stop=(g == NG - 1 and t == 3),
+                    )
 
-        def passes_last(g):
-            for i in range(2):
-                one_pass(q_last[i][:], g, last, half * i, half)
-
-        q_sb = {}
-
-        def copy_out(grp):
-            qb = keep.tile([P, K_PASS], BF16, name="q%d" % grp)
-            q_sb[grp] = (qb, 0)
-            if grp < last:
-                copy = scopy if grp % 2 == 0 else vcopy
-                copy(out=qb[:], in_=qps[grp][:])
-            else:
-                scopy(out=qb[:, :half], in_=q_last[0][:])
-                vcopy(out=qb[:, half:], in_=q_last[1][:])
+        def copy_out(copy, grp):
+            copy(out=qg[:, grp, :, :], in_=qps[grp][:].rearrange("p t j -> p j t"))
 
         accs = []
 
@@ -180,54 +185,37 @@ def tile_bilinear_w_kernel(tc, tensor0, tensor1, kernel_words, kernel_scales, bi
                     stop=(grp == NG - 1),
                 )
 
+        def sort_and_pass(g, first, groups):
+            sort_w(g, first, groups)
+            passes(g, range(first, first + groups))
+
         for g in range(4):
-            passes(g, range(last))
+            sort_and_pass(g, 0, 4)
+            sort_and_pass(g, 4, 4)
         for g in range(4, NG):
-            passes(g, range(4))
+            sort_and_pass(g, 0, 4)
         for grp in range(4):
-            copy_out(grp)
-        for i, b in enumerate((3, 7)):
-            ql = bank(b, [P, half], "q_last%d" % i)
-            q_last.append(ql)
-        for g in range(4):
-            passes_last(g)
-        passes(4, range(4, last))
-        passes_last(4)
-        xq01 = transposes(0, (0, 1), q_sb, "xq01")
-        xq23 = transposes(1, (2, 3), q_sb, "xq23")
-        lay_out(scopy, qg, (0, 1), xq01)
-        lay_out(vcopy, qg, (2, 3), xq23)
-        quantise(qc, qs, qg, 0, 2)
-        quantise(qc, qs, qg, 2, 2)
-        passes(5, range(4, last))
-        passes_last(5)
-        acc = bank(2, [P, P], "acc")
+            copy_out(scopy, grp)
+        acc = bank(0, [P, P], "acc")
         accs.append(acc)
+        sort_and_pass(4, 4, 4)
+        quantise(qc, qs, qg, 0, 4)
+        sort_and_pass(5, 4, 4)
         second_stage(range(4))
 
-        passes(6, (4, 5))
-        passes(7, (4, 5))
-        copy_out(4)
-        copy_out(5)
-        passes(6, (6,))
-        passes_last(6)
-        passes(7, (6,))
-        copy_out(6)
-        xq4 = transposes(0, (4,), q_sb, "xq4")
-        xq5 = transposes(1, (5,), q_sb, "xq5")
-        lay_out(scopy, qg, (4,), xq4)
-        lay_out(vcopy, qg, (5,), xq5)
-        passes_last(7)
-        copy_out(7)
+        sort_and_pass(6, 4, 2)
+        sort_and_pass(7, 4, 2)
+        copy_out(scopy, 4)
+        copy_out(scopy, 5)
+        sort_and_pass(6, 6, 2)
+        sort_and_pass(7, 6, 1)
+        copy_out(scopy, 6)
+        sort_and_pass(7, 7, 1)
         quantise(qc, qs, qg, 4, 2)
-        xq6 = transposes(4, (6,), q_sb, "xq6")
-        lay_out(scopy, qg, (6,), xq6)
-        xq7 = transposes(5, (7,), q_sb, "xq7")
-        lay_out(scopy, qg, (7,), xq7)
-        second_stage((4, 5))
+        copy_out(vcopy, 7)
         quantise(qc, qs, qg, 6, 1)
         quantise(qc, qs, qg, 7, 1)
-        second_stage((6, 7))
+        second_stage(range(4, 8))
 
         res = keep.tile([P, P], F32)
         nc.vector.tensor_scalar_add(out=res[:], in0=acc[:], scalar1=bias32[:, 0:1])

@@ -196,26 +196,29 @@ def tile_bilinear_w_kernel(tc, tensor0, tensor1, kernel_words, kernel_scales, bi
             sort_and_pass(g, 0, 4)
         for grp in range(4):
             copy_out(scopy, grp)
-        acc = bank(0, [P, P], "acc")
-        accs.append(acc)
         sort_and_pass(4, 4, 4)
-        quantise(qc, qs, qg, 0, 4)
-        sort_and_pass(5, 4, 4)
-        second_stage(range(4))
-
-        sort_and_pass(6, 4, 2)
-        sort_and_pass(7, 4, 2)
-        copy_out(scopy, 4)
-        copy_out(scopy, 5)
-        sort_and_pass(6, 6, 2)
+        quantise(qc, qs, qg, 0, 2)
+        for first in (4, 6):
+            sort_and_pass(5, first, 2)
+        for grp in (4, 5):
+            sort_and_pass(6, grp, 1)
+        quantise(qc, qs, qg, 2, 2)
+        for grp in (4, 5):
+            sort_and_pass(7, grp, 1)
+            copy_out(scopy, grp)
+        for grp in (6, 7):
+            sort_and_pass(6, grp, 1)
         sort_and_pass(7, 6, 1)
         copy_out(scopy, 6)
         sort_and_pass(7, 7, 1)
         quantise(qc, qs, qg, 4, 2)
+        acc = bank(0, [P, P], "acc")
+        accs.append(acc)
+        second_stage(range(6))
         copy_out(vcopy, 7)
         quantise(qc, qs, qg, 6, 1)
         quantise(qc, qs, qg, 7, 1)
-        second_stage(range(4, 8))
+        second_stage((6, 7))
 
         res = keep.tile([P, P], F32)
         nc.vector.tensor_scalar_add(out=res[:], in0=acc[:], scalar1=bias32[:, 0:1])

@@ -46,8 +46,6 @@ def tile_bilinear_w_kernel(tc, tensor0, tensor1, kernel_words, kernel_scales, bi
         t0_sb = keep.tile([P, D], BF16)
         nc.sync.dma_start(out=t0_sb[:], in_=tensor0[0, :, :])
         nc.sync.dma_start(out=brow[0:1, 0:1], in_=bias.unsqueeze(0))
-        t1_sb = keep.tile([P, D], BF16)
-        nc.sync.dma_start(out=t1_sb[:], in_=tensor1[0, :, :])
 
         ks = kernel_scales.bitcast(I32)
         for h in range(2):
@@ -57,6 +55,9 @@ def tile_bilinear_w_kernel(tc, tensor0, tensor1, kernel_words, kernel_scales, bi
                         out=wsc[32 * quad : 32 * quad + 16, h, 2048 * half : 2048 * (half + 1)].bitcast(I32),
                         in_=ks[4 * h : 4 * h + 4, 4 * quad : 4 * quad + 4, 512 * half : 512 * (half + 1)],
                     )
+
+        t1_sb = keep.tile([P, D], BF16)
+        nc.sync.dma_start(out=t1_sb[:], in_=tensor1[0, :, :])
 
         kw = kernel_words.rearrange("g p n t -> g p (n t)").bitcast(I32)
         w_raw = {}

@@ -15,6 +15,9 @@ D = 4096
 K_PASS = 512
 NG = D // K_PASS
 
+RAW_BUFS = {8: 4, 4: 4, 2: 3, 1: 2}
+SORTED_BUFS = {4: 3, 2: 2, 1: 4}
+
 FLOPS = 2 * P * D * D + 2 * P * P * D
 
 
@@ -22,8 +25,8 @@ def tile_bilinear_w_kernel(tc, tensor0, tensor1, kernel_words, kernel_scales, bi
     nc = tc.nc
     with ExitStack() as ctx:
         keep = ctx.enter_context(tc.tile_pool(name="keep", bufs=1))
-        raw = ctx.enter_context(tc.tile_pool(name="raw", bufs=5))
-        sorted_w = ctx.enter_context(tc.tile_pool(name="sorted", bufs=4))
+        raw = ctx.enter_context(tc.tile_pool(name="raw", bufs=4))
+        sorted_w = ctx.enter_context(tc.tile_pool(name="sorted", bufs=3))
         psum = ctx.enter_context(tc.psum_pool(name="psum", bufs=1))
         ctx.enter_context(tc.manual_schedule())
         vcopy, scopy = nc.vector.tensor_copy, nc.scalar.copy
@@ -64,7 +67,7 @@ def tile_bilinear_w_kernel(tc, tensor0, tensor1, kernel_words, kernel_scales, bi
 
         def load_w(g, first_group, groups):
             n0, cols = K_PASS * first_group, K_PASS * groups
-            wt = raw.tile([P, cols], I32, tag="raw", name="w%d_%d" % (g, first_group), align_bytes=64)
+            wt = raw.tile([P, cols], I32, tag="raw%d" % groups, bufs=RAW_BUFS[groups], name="w%d_%d" % (g, first_group), align_bytes=64)
             nc.sync.dma_start(out=wt[:], in_=kw[g, :, n0 : n0 + cols])
             for j in range(groups):
                 w_raw[(g, first_group + j)] = (wt, K_PASS * j)
@@ -145,7 +148,7 @@ def tile_bilinear_w_kernel(tc, tensor0, tensor1, kernel_words, kernel_scales, bi
         def sort_w(g, first_group, groups):
             wt, off = w_raw[(g, first_group)]
             cols = P * groups
-            ws = sorted_w.tile([P, 4, cols], I32, tag="s%d" % groups, name="s%d_%d" % (g, first_group), align_bytes=64)
+            ws = sorted_w.tile([P, 4, cols], I32, tag="s%d" % groups, bufs=SORTED_BUFS[groups], name="s%d_%d" % (g, first_group), align_bytes=64)
             vcopy(
                 out=ws[:].rearrange("p t (b r) -> p t b r", r=8),
                 in_=wt[:, off : off + 4 * cols].rearrange("p (b t r) -> p t b r", t=4, r=8),
@@ -210,13 +213,13 @@ def tile_bilinear_w_kernel(tc, tensor0, tensor1, kernel_words, kernel_scales, bi
         for grp in (6, 7):
             sort_and_pass(6, grp, 1)
         sort_and_pass(7, 6, 1)
-        copy_out(scopy, 6)
         sort_and_pass(7, 7, 1)
+        copy_out(vcopy, 6)
         quantise(qc, qs, qg, 4, 2)
         acc = bank(0, [P, P], "acc")
         accs.append(acc)
         second_stage(range(6))
-        copy_out(vcopy, 7)
+        copy_out(scopy, 7)
         quantise(qc, qs, qg, 6, 1)
         quantise(qc, qs, qg, 7, 1)
         second_stage((6, 7))

@@ -52,12 +52,11 @@ def tile_bilinear_w_kernel(tc, tensor0, tensor1, kernel_words, kernel_scales, bi
 
         ks = kernel_scales.bitcast(I32)
         for h in range(2):
-            for half in range(2):
-                for quad in (0, 2, 1, 3):
-                    nc.sync.dma_start(
-                        out=wsc[32 * quad : 32 * quad + 16, h, 2048 * half : 2048 * (half + 1)].bitcast(I32),
-                        in_=ks[4 * h : 4 * h + 4, 4 * quad : 4 * quad + 4, 512 * half : 512 * (half + 1)],
-                    )
+            for quad in (0, 2, 1, 3):
+                nc.sync.dma_start(
+                    out=wsc[32 * quad : 32 * quad + 16, h, :].bitcast(I32),
+                    in_=ks[4 * h : 4 * h + 4, 4 * quad : 4 * quad + 4, :],
+                )
 
         t1_sb = keep.tile([P, D], BF16)
         nc.sync.dma_start(out=t1_sb[:], in_=tensor1[0, :, :])

@@ -51,8 +51,8 @@ def tile_bilinear_w_kernel(tc, tensor0, tensor1, kernel_words, kernel_scales, bi
         nc.sync.dma_start(out=brow[0:1, 0:1], in_=bias.unsqueeze(0))
 
         ks = kernel_scales.bitcast(I32)
-        for h in range(2):
-            for quad in (0, 2, 1, 3):
+        for quad in (2, 3, 0, 1):
+            for h in range(2):
                 nc.sync.dma_start(
                     out=wsc[32 * quad : 32 * quad + 16, h, :].bitcast(I32),
                     in_=ks[4 * h : 4 * h + 4, 4 * quad : 4 * quad + 4, :],

from contextlib import ExitStack

import concourse.mybir as mybir
from concourse.masks import make_identity

F32 = mybir.dt.float32
BF16 = mybir.dt.bfloat16
I32 = mybir.dt.int32
U32 = mybir.dt.uint32
U8 = mybir.dt.uint8
FP8X4 = mybir.dt.float8_e4m3fn_x4

P = 128
D = 4096
K_PASS = 512
NG = D // K_PASS

RAW_BUFS = {8: 4, 4: 4, 2: 3, 1: 2}
SORTED_BUFS = {4: 3, 2: 2, 1: 4}

FLOPS = 2 * P * D * D + 2 * P * P * D


def tile_bilinear_w_kernel(tc, tensor0, tensor1, kernel_words, kernel_scales, bias, out):
    nc = tc.nc
    with ExitStack() as ctx:
        keep = ctx.enter_context(tc.tile_pool(name="keep", bufs=1))
        raw = ctx.enter_context(tc.tile_pool(name="raw", bufs=4))
        sorted_w = ctx.enter_context(tc.tile_pool(name="sorted", bufs=3))
        psum = ctx.enter_context(tc.psum_pool(name="psum", bufs=1))
        ctx.enter_context(tc.manual_schedule())
        vcopy, scopy = nc.vector.tensor_copy, nc.scalar.copy

        def bank(i, shape, name, dtype=F32):
            return psum.tile(shape, dtype, tag="bank%d" % i, name=name)

        brow = keep.tile([P, 32], BF16)
        nc.vector.memset(brow[:], 0.0)
        wsc = keep.tile([P, 2, D], U8, align_bytes=64)
        nc.vector.memset(wsc[:].rearrange("p h n -> p (h n)").bitcast(I32), 0)
        ones = keep.tile([P, P], BF16)
        nc.vector.memset(ones[:], 1.0)

        ident32 = keep.tile([P, P], F32)
        make_identity(nc, ident32[:])
        identb = keep.tile([P, P], BF16)
        make_identity(nc, identb[:])

        t0_sb = keep.tile([P, D], BF16)
        nc.sync.dma_start(out=t0_sb[:], in_=tensor0[0, :, :])
        nc.sync.dma_start(out=brow[0:1, 0:1], in_=bias.unsqueeze(0))

        ks = kernel_scales.bitcast(I32)
        for quad in (2, 3, 0, 1):
            for h in range(2):
                nc.sync.dma_start(
                    out=wsc[32 * quad : 32 * quad + 16, h, :].bitcast(I32),
                    in_=ks[4 * h : 4 * h + 4, 4 * quad : 4 * quad + 4, :],
                )

        t1_sb = keep.tile([P, D], BF16)
        nc.sync.dma_start(out=t1_sb[:], in_=tensor1[0, :, :])

        kw = kernel_words.rearrange("g p n t -> g p (n t)").bitcast(I32)
        w_raw = {}

        def load_w(g, first_group, groups):
            n0, cols = K_PASS * first_group, K_PASS * groups
            wt = raw.tile([P, cols], I32, tag="raw%d" % groups, bufs=RAW_BUFS[groups], name="w%d_%d" % (g, first_group), align_bytes=64)
            nc.sync.dma_start(out=wt[:], in_=kw[g, :, n0 : n0 + cols])
            for j in range(groups):
                w_raw[(g, first_group + j)] = (wt, K_PASS * j)

        for g in range(4):
            load_w(g, 0, 8)
        for g in range(4, NG):
            load_w(g, 0, 4)
        for g in (4, 5):
            load_w(g, 4, 4)
        for g in (6, 7):
            load_w(g, 4, 2)
        load_w(6, 6, 2)
        load_w(7, 6, 1)
        load_w(7, 7, 1)

        def quantise(codes, scales, grouped, first, groups):
            sl = slice(first, first + groups)
            nc.vector.quantize_mx(
                out=codes[:, sl, :].rearrange("p g j -> p (g j)").bitcast(FP8X4),
                scales=scales[:, sl, :].rearrange("p g j -> p (g j)"),
                in_=grouped[:, sl, :, :].rearrange("p g j t -> p (g j t)"),
            )

        def operand(name):
            grouped = keep.tile([P, NG, P, 4], BF16, align_bytes=64, name=name + "g")
            codes = keep.tile([P, NG, P], U32, align_bytes=64, name=name + "c")
            scales = keep.tile([P, NG, P], U8, align_bytes=64, name=name + "s")
            return grouped, codes, scales

        t0g, t0c, t0s = operand("t0")
        t1g, t1c, t1s = operand("t1")
        qg, qc, qs = operand("q")

        words = t0_sb[:].bitcast(F32)
        for pair in range(4):
            xt0 = bank(pair, [P, 2, 2, P], "xt0_%d" % pair)
            for i in range(2):
                w0 = 256 * (2 * pair + i)
                for u in range(2):
                    nc.tensor.transpose(out=xt0[:, i, u, :], in_=words[:, w0 + u : w0 + 256 : 2], identity=ident32[:])
            copy = vcopy if pair % 2 == 0 else scopy
            copy(
                out=t0g[:].bitcast(F32)[:, 2 * pair : 2 * pair + 2, :, :],
                in_=xt0[:].rearrange("p g u j -> p g j u"),
            )
        quantise(t0c, t0s, t0g, 0, 4)
        quantise(t0c, t0s, t0g, 4, 4)

        bps = bank(6, [P, 32], "bps")
        nc.tensor.matmul(out=bps[:], lhsT=ones[:], rhs=brow[:], start=True, stop=True)
        bias32 = keep.tile([P, 1], F32)
        scopy(out=bias32[:], in_=bps[:, 0:1])

        t1_sorted = keep.tile([P, 4, P, 4], F32)
        vcopy(out=t1_sorted[:], in_=t1_sb[:].bitcast(F32).rearrange("p (b t r) -> p t b r", t=4, r=4))
        t1_cols = t1_sorted[:].rearrange("p t b r -> p (t b r)").bitcast(BF16)
        for pair, b in enumerate((4, 5, 7, 0)):
            xt1 = bank(b, [P, 2, 4, P], "xt1_%d" % pair, BF16)
            for i in range(2):
                for t in range(4):
                    c0 = D // 4 * t + P * (2 * pair + i)
                    nc.tensor.transpose(out=xt1[:, i, t, :], in_=t1_cols[:, c0 : c0 + P], identity=identb[:])
            copy = scopy if pair % 2 == 0 else vcopy
            copy(out=t1g[:, 2 * pair : 2 * pair + 2, :, :], in_=xt1[:].rearrange("p g t i -> p g i t"))
        quantise(t1c, t1s, t1g, 0, 4)
        quantise(t1c, t1s, t1g, 4, 4)

        wss = keep.tile([P, 2, 4, D // 4], U8, align_bytes=64)
        for h in range(2):
            vcopy(
                out=wss[:, h, :, :].rearrange("p t c -> p (t c)").bitcast(I32).rearrange("p (t b r) -> p t b r", t=4, r=2),
                in_=wsc[:, h, :].bitcast(I32).rearrange("p (b t r) -> p t b r", t=4, r=2),
            )

        w_at = {}

        def sort_w(g, first_group, groups):
            wt, off = w_raw[(g, first_group)]
            cols = P * groups
            ws = sorted_w.tile([P, 4, cols], I32, tag="s%d" % groups, bufs=SORTED_BUFS[groups], name="s%d_%d" % (g, first_group), align_bytes=64)
            vcopy(
                out=ws[:].rearrange("p t (b r) -> p t b r", r=8),
                in_=wt[:, off : off + 4 * cols].rearrange("p (b t r) -> p t b r", t=4, r=8),
            )
            for j in range(groups):
                w_at[(g, first_group + j)] = (ws, P * j)

        qps = [bank(grp, [P, 4, P], "qps%d" % grp) for grp in range(NG)]

        def passes(g, groups):
            for grp in groups:
                ws, c0 = w_at[(g, grp)]
                for t in range(4):
                    nc.tensor.matmul_mx(
                        out=qps[grp][:, t, :],
                        lhsT=ws[:, t, c0 : c0 + P].bitcast(FP8X4),
                        lhsT_scale=wss[4 * (g % 4) : P, g // 4, t, P * grp : P * (grp + 1)],
                        rhs=t0c[:, g, :].bitcast(FP8X4),
                        rhs_scale=t0s[:, g, :],
                        start=(g == 0 and t == 0),
                        stop=(g == NG - 1 and t == 3),
                    )

        def copy_out(copy, grp):
            copy(out=qg[:, grp, :, :], in_=qps[grp][:].rearrange("p t j -> p j t"))

        accs = []

        def second_stage(groups):
            for grp in groups:
                nc.tensor.matmul_mx(
                    out=accs[0][:],
                    lhsT=t1c[:, grp, :].bitcast(FP8X4),
                    lhsT_scale=t1s[:, grp, :],
                    rhs=qc[:, grp, :].bitcast(FP8X4),
                    rhs_scale=qs[:, grp, :],
                    start=(grp == 0),
                    stop=(grp == NG - 1),
                )

        def sort_and_pass(g, first, groups):
            sort_w(g, first, groups)
            passes(g, range(first, first + groups))

        for g in range(4):
            sort_and_pass(g, 0, 4)
            sort_and_pass(g, 4, 4)
        for g in range(4, NG):
            sort_and_pass(g, 0, 4)
        for grp in range(4):
            copy_out(scopy, grp)
        sort_and_pass(4, 4, 4)
        quantise(qc, qs, qg, 0, 2)
        for first in (4, 6):
            sort_and_pass(5, first, 2)
        for grp in (4, 5):
            sort_and_pass(6, grp, 1)
        quantise(qc, qs, qg, 2, 2)
        for grp in (4, 5):
            sort_and_pass(7, grp, 1)
            copy_out(scopy, grp)
        for grp in (6, 7):
            sort_and_pass(6, grp, 1)
        sort_and_pass(7, 6, 1)
        sort_and_pass(7, 7, 1)
        copy_out(vcopy, 6)
        quantise(qc, qs, qg, 4, 2)
        acc = bank(0, [P, P], "acc")
        accs.append(acc)
        second_stage(range(6))
        copy_out(scopy, 7)
        quantise(qc, qs, qg, 6, 1)
        quantise(qc, qs, qg, 7, 1)
        second_stage((6, 7))

        res = keep.tile([P, P], F32)
        nc.vector.tensor_scalar_add(out=res[:], in0=acc[:], scalar1=bias32[:, 0:1])
        nc.sync.dma_start(out=out[0, 0, :, :], in_=res[:])
        nc.scalar.dma_start(out=out[1, 0, :, :], in_=res[:])
